import numpy as np
import ml_dtypes


def mxq(x, axis, fmt="e4m3"):
    dtype, down = {"e4m3": (ml_dtypes.float8_e4m3fn, 7), "e5m2": (ml_dtypes.float8_e5m2, 14)}[fmt]
    v = np.moveaxis(np.asarray(x, np.float32).astype(ml_dtypes.bfloat16).astype(np.float64), axis, -1)
    blocks = v.reshape(v.shape[:-1] + (-1, 32))
    amax = np.abs(blocks).max(-1, keepdims=True)
    byte = np.maximum(np.where(amax > 0, np.frexp(amax)[1] - 1 + 127, 0) - down, 1)
    scale = np.exp2(byte - 127.0)
    codes = (blocks / scale).astype(np.float32).astype(dtype).astype(np.float64)
    return np.moveaxis((codes * scale).reshape(v.shape), -1, axis)


WIDE = False


def mx_kscale(k):
    if not WIDE:
        return np.ones(k)
    levels = np.array([10, -10, 5, -5, 0])
    a = np.random.permutation(np.resize(levels, k // 512 * 4)).reshape(k // 512, 4)
    idx = np.arange(k)
    return np.exp2(a[idx // 512, idx % 128 // 32])


BF16 = ml_dtypes.bfloat16


def bf(x):
    return np.asarray(x, np.float32).astype(BF16)


def f64(x):
    return np.asarray(x).astype(np.float64)


E2M1 = np.array([0.0, 0.5, 1.0, 1.5, 2.0, 3.0, 4.0, 6.0, -0.0, -0.5, -1.0, -1.5, -2.0, -3.0, -4.0, -6.0])


def pack_weight(w, fmt):
    k, n = w.shape
    w = f64(bf(w)).reshape(k // 32, 32, n)
    amax = np.abs(w).max(1)
    if fmt == "e4m3":
        byte = np.frexp(amax)[1] - 1 + 127 - 7
    else:
        mant, ex = np.frexp(amax / 6.0)
        byte = np.where(mant > 0.5, ex, ex - 1) + 127
    byte = np.clip(np.where(amax > 0, byte, 1), 1, 254)
    scaled = (w * np.exp2(127.0 - byte)[:, None, :]).reshape(k, n).astype(np.float32)
    by_word = np.ascontiguousarray(scaled.reshape(k // 512, 128, 4, n).transpose(0, 1, 3, 2))
    if fmt == "e4m3":
        words = by_word.astype(ml_dtypes.float8_e4m3fn).view(np.uint8)
    else:
        c = by_word.astype(ml_dtypes.float4_e2m1fn).view(np.uint8) & 0xF
        words = c[..., 0::2] | (c[..., 1::2] << 4)
    return np.ascontiguousarray(words), np.ascontiguousarray(byte.astype(np.uint8).reshape(k // 512, 16, n))


def unpack_weight(words, scales, fmt):
    g, p, n, _ = words.shape
    if fmt == "e4m3":
        vals = np.ascontiguousarray(words).view(ml_dtypes.float8_e4m3fn).astype(np.float64)
    else:
        nib = np.empty((g, p, n, 4), np.uint8)
        nib[..., 0::2] = words & 0xF
        nib[..., 1::2] = words >> 4
        vals = E2M1[nib]
    vals = vals * np.repeat(np.exp2(scales.astype(np.float64) - 127.0), 8, axis=1)[..., None]
    return vals.transpose(0, 1, 3, 2).reshape(g * 512, n)


B, DIN, F, NCLS, NV = 128, 2048, 1024, 18, 3
S_NM = 2.0 / np.sqrt(DIN)
S_AN = 0.25 * np.sqrt(F / DIN)
FMT = "e4m3"


def draw_view():
    s = mx_kscale(DIN)
    x = bf(np.random.standard_normal((B, DIN)) * s)
    nm_words, nm_scales = pack_weight(np.random.standard_normal((DIN, F)) * S_NM / s[:, None], FMT)
    an_words, an_scales = pack_weight(np.random.standard_normal((DIN, F)) * S_AN / s[:, None], FMT)
    return x, nm_words, nm_scales, an_words, an_scales


def setup_inputs():
    x_dash, Wd_nm_words, Wd_nm_scales, Wd_an_words, Wd_an_scales = draw_view()
    x_rear, Wr_nm_words, Wr_nm_scales, Wr_an_words, Wr_an_scales = draw_view()
    x_right, Wt_nm_words, Wt_nm_scales, Wt_an_words, Wt_an_scales = draw_view()
    return {"x_dash": x_dash, "x_rear": x_rear, "x_right": x_right,
            "Wd_nm_words": Wd_nm_words, "Wd_nm_scales": Wd_nm_scales,
            "Wd_an_words": Wd_an_words, "Wd_an_scales": Wd_an_scales,
            "Wr_nm_words": Wr_nm_words, "Wr_nm_scales": Wr_nm_scales,
            "Wr_an_words": Wr_an_words, "Wr_an_scales": Wr_an_scales,
            "Wt_nm_words": Wt_nm_words, "Wt_nm_scales": Wt_nm_scales,
            "Wt_an_words": Wt_an_words, "Wt_an_scales": Wt_an_scales}


def branch(x, nm_words, nm_scales, an_words, an_scales):
    xq = mxq(f64(x), 1, "e4m3")
    nm = xq @ unpack_weight(nm_words, nm_scales, FMT)
    an = xq @ unpack_weight(an_words, an_scales, FMT)
    return np.mean(an, axis=1, keepdims=True) * nm


def reference(x_dash, x_rear, x_right, Wd_nm_words, Wd_nm_scales, Wd_an_words, Wd_an_scales, Wr_nm_words, Wr_nm_scales, Wr_an_words, Wr_an_scales, Wt_nm_words, Wt_nm_scales, Wt_an_words, Wt_an_scales):
    v = np.concatenate([branch(x_dash, Wd_nm_words, Wd_nm_scales, Wd_an_words, Wd_an_scales), branch(x_rear, Wr_nm_words, Wr_nm_scales, Wr_an_words, Wr_an_scales), branch(x_right, Wt_nm_words, Wt_nm_scales, Wt_an_words, Wt_an_scales)], axis=1)
    return v.reshape(v.shape[0], F, NV).mean(axis=-1)

@@ -1,0 +1,170 @@
+from contextlib import ExitStack
+
+import concourse.mybir as mybir
+from concourse.masks import make_identity
+
+F32 = mybir.dt.float32
+BF16 = mybir.dt.bfloat16
+I32 = mybir.dt.int32
+U32 = mybir.dt.uint32
+U8 = mybir.dt.uint8
+FP8X4 = mybir.dt.float8_e4m3fn_x4
+ADD = mybir.AluOpType.add
+MULT = mybir.AluOpType.mult
+
+P = 128
+PACK = 4
+K = 2048
+K_PASS = P * PACK
+PASSES = K // K_PASS
+F = 1024
+BANK = 512
+HALVES = F // BANK
+VIEWS = 3
+WEIGHTS = 2 * VIEWS
+MERGE = 3
+WORDS_PASS = K_PASS // 2
+QUADRANT = 32
+SCALE_ROWS = 4
+STORE_STEP = 8
+
+FLOPS = 2 * P * K * F * WEIGHTS
+
+
+def columns_of_out_ready(banks_done):
+    return (banks_done * BANK // MERGE) // STORE_STEP * STORE_STEP
+
+
+def tile_fusion_r3d_pa_kernel(
+    tc,
+    x_dash, x_rear, x_right,
+    Wd_nm_words, Wd_nm_scales, Wd_an_words, Wd_an_scales,
+    Wr_nm_words, Wr_nm_scales, Wr_an_words, Wr_an_scales,
+    Wt_nm_words, Wt_nm_scales, Wt_an_words, Wt_an_scales,
+    out,
+):
+    nc = tc.nc
+    xs = [x_dash, x_rear, x_right]
+    weights = [
+        (Wd_an_words, Wd_an_scales), (Wd_nm_words, Wd_nm_scales),
+        (Wr_an_words, Wr_an_scales), (Wr_nm_words, Wr_nm_scales),
+        (Wt_an_words, Wt_an_scales), (Wt_nm_words, Wt_nm_scales),
+    ]
+
+    with ExitStack() as ctx:
+        keep = ctx.enter_context(tc.tile_pool(name="keep", bufs=1))
+        xt_pool = ctx.enter_context(tc.psum_pool(name="xt_pool", bufs=4))
+        acc_pool = ctx.enter_context(tc.psum_pool(name="acc_pool", bufs=1))
+        ctx.enter_context(tc.manual_schedule())
+
+        ident = keep.tile([P, P], F32)
+        x_sb = [keep.tile([P, K], BF16, name="x_sb%d" % view) for view in range(VIEWS)]
+        w_words = [keep.tile([P, PASSES, F], U32, name="w_words%d" % w, align_bytes=64)
+                   for w in range(WEIGHTS)]
+        w_scales = keep.tile([P, WEIGHTS, F], U8, align_bytes=64)
+        v = keep.tile([P, VIEWS * F], F32)
+        out_sb = keep.tile([P, F], F32)
+
+        make_identity(nc, ident[:])
+        nc.vector.memset(w_scales[:].rearrange("p w n -> p (w n)").bitcast(I32), 0)
+
+        for view in range(VIEWS):
+            nc.sync.dma_start(out=x_sb[view][:], in_=xs[view])
+        for w in range(WEIGHTS):
+            scale_rows = weights[w][1].bitcast(I32)
+            for quad in range(P // QUADRANT):
+                top = quad * QUADRANT
+                nc.sync.dma_start(
+                    out=w_scales[top : top + PASSES * SCALE_ROWS, w, :].bitcast(I32),
+                    in_=scale_rows[:, quad * SCALE_ROWS : (quad + 1) * SCALE_ROWS, :],
+                )
+        for w in range(WEIGHTS):
+            for g in range(PASSES):
+                nc.sync.dma_start(
+                    out=w_words[w][:, g, :].bitcast(I32),
+                    in_=weights[w][0][g].rearrange("p n t -> p (n t)").bitcast(I32),
+                )
+
+        x_codes = []
+        x_scales = []
+        for view in range(VIEWS):
+            x_words = x_sb[view][:].bitcast(F32)
+            grouped = keep.tile([P, PASSES, P, PACK], BF16, name="grouped%d" % view, align_bytes=64)
+            grouped_words = (
+                grouped[:].rearrange("p g b t -> p (g b t)").bitcast(F32)
+                .rearrange("p (g b u) -> p g b u", g=PASSES, u=2)
+            )
+            for pair in range(PASSES // 2):
+                xt = xt_pool.tile([P, 2, 2, P], F32)
+                for i in range(2):
+                    g = 2 * pair + i
+                    for u in range(2):
+                        nc.tensor.transpose(
+                            xt[:, i, u, :],
+                            x_words[:, g * WORDS_PASS + u : (g + 1) * WORDS_PASS : 2],
+                            ident[:],
+                        )
+                copy_out = nc.scalar.copy if pair == 0 else nc.vector.tensor_copy
+                copy_out(
+                    out=grouped_words[:, 2 * pair : 2 * pair + 2, :, :],
+                    in_=xt[:].rearrange("p i u b -> p i b u"),
+                )
+            codes = keep.tile([P, PASSES * P], U32, name="x_codes%d" % view, align_bytes=64)
+            scales = keep.tile([P, PASSES * P], U8, name="x_scales%d" % view, align_bytes=64)
+            nc.vector.quantize_mx(
+                out=codes[:].bitcast(FP8X4),
+                scales=scales[:],
+                in_=grouped[:].rearrange("p g b t -> p (g b t)"),
+            )
+            x_codes.append(codes)
+            x_scales.append(scales)
+
+        def multiply(view, w, tag):
+            acc = [acc_pool.tile([P, BANK], F32, name="%s%d" % (tag, h)) for h in range(HALVES)]
+            for g in range(PASSES):
+                rows = slice(g * P, (g + 1) * P)
+                for h in range(HALVES):
+                    cols = slice(h * BANK, (h + 1) * BANK)
+                    nc.tensor.matmul_mx(
+                        out=acc[h][:],
+                        lhsT=x_codes[view][:, rows].bitcast(FP8X4),
+                        lhsT_scale=x_scales[view][:, rows],
+                        rhs=w_words[w][:, g, cols].bitcast(FP8X4),
+                        rhs_scale=w_scales[g * SCALE_ROWS : P, w, cols],
+                        start=(g == 0),
+                        stop=(g == PASSES - 1),
+                    )
+            return acc
+
+        for view in range(VIEWS):
+            an = multiply(view, 2 * view, "an")
+            an_sum = keep.tile([P, HALVES], F32, name="an_sum%d" % view)
+            for h in range(HALVES):
+                nc.vector.tensor_reduce(
+                    out=an_sum[:, h : h + 1], in_=an[h][:], axis=mybir.AxisListType.X, op=ADD
+                )
+            gate = keep.tile([P, 1], F32, name="gate%d" % view)
+            nc.vector.tensor_scalar(
+                out=gate[:], in0=an_sum[:, 0:1], scalar1=an_sum[:, 1:2],
+                scalar2=1.0 / (F * MERGE), op0=ADD, op1=MULT,
+            )
+
+            nm = multiply(view, 2 * view + 1, "nm")
+            first = view * F
+            nc.scalar.activation(
+                out=v[:, first : first + BANK], in_=nm[0][:],
+                func=mybir.ActivationFunctionType.Copy, scale=gate[:, 0:1],
+            )
+            nc.vector.tensor_scalar(
+                out=v[:, first + BANK : first + F], in0=nm[1][:], scalar1=gate[:, 0:1],
+                scalar2=None, op0=MULT,
+            )
+
+            j0 = columns_of_out_ready(view * HALVES)
+            j1 = columns_of_out_ready((view + 1) * HALVES)
+            nc.vector.tensor_reduce(
+                out=out_sb[:, j0:j1],
+                in_=v[:, MERGE * j0 : MERGE * j1].rearrange("p (j t) -> p j t", t=MERGE),
+                axis=mybir.AxisListType.X, op=ADD,
+            )
+            nc.sync.dma_start(out=out[:, j0:j1], in_=out_sb[:, j0:j1])

@@ -68,9 +68,10 @@ def tile_fusion_r3d_pa_kernel(
         make_identity(nc, ident[:])
         nc.vector.memset(w_scales[:].rearrange("p w n -> p (w n)").bitcast(I32), 0)
 
-        for view in range(VIEWS):
+        def load_x(view):
             nc.sync.dma_start(out=x_sb[view][:], in_=xs[view])
-        for w in range(WEIGHTS):
+
+        def load_scales(w):
             scale_rows = weights[w][1].bitcast(I32)
             for quad in range(P // QUADRANT):
                 top = quad * QUADRANT
@@ -78,12 +79,22 @@ def tile_fusion_r3d_pa_kernel(
                     out=w_scales[top : top + PASSES * SCALE_ROWS, w, :].bitcast(I32),
                     in_=scale_rows[:, quad * SCALE_ROWS : (quad + 1) * SCALE_ROWS, :],
                 )
-        for w in range(WEIGHTS):
+
+        def load_words(w):
             for g in range(PASSES):
                 nc.sync.dma_start(
                     out=w_words[w][:, g, :].bitcast(I32),
                     in_=weights[w][0][g].rearrange("p n t -> p (n t)").bitcast(I32),
                 )
+
+        load_x(0)
+        load_scales(0)
+        load_x(1)
+        load_x(2)
+        for w in range(WEIGHTS):
+            if w + 1 < WEIGHTS:
+                load_scales(w + 1)
+            load_words(w)
 
         x_codes = []
         x_scales = []

@@ -82,10 +82,14 @@ def tile_fusion_r3d_pa_kernel(
 
         def load_words(w):
             for g in range(PASSES):
-                nc.sync.dma_start(
-                    out=w_words[w][:, g, :].bitcast(I32),
-                    in_=weights[w][0][g].rearrange("p n t -> p (n t)").bitcast(I32),
-                )
+                is_last_load = w == WEIGHTS - 1 and g == PASSES - 1
+                width = BANK if is_last_load else F
+                for left in range(0, F, width):
+                    nc.sync.dma_start(
+                        out=w_words[w][:, g, left : left + width].bitcast(I32),
+                        in_=weights[w][0][g, :, left : left + width, :]
+                        .rearrange("p n t -> p (n t)").bitcast(I32),
+                    )
 
         load_x(0)
         load_scales(0)
@@ -161,21 +165,17 @@ def tile_fusion_r3d_pa_kernel(
             )
 
             nm = multiply(view, 2 * view + 1, "nm")
-            first = view * F
-            nc.scalar.activation(
-                out=v[:, first : first + BANK], in_=nm[0][:],
-                func=mybir.ActivationFunctionType.Copy, scale=gate[:, 0:1],
-            )
-            nc.vector.tensor_scalar(
-                out=v[:, first + BANK : first + F], in0=nm[1][:], scalar1=gate[:, 0:1],
-                scalar2=None, op0=MULT,
-            )
-
-            j0 = columns_of_out_ready(view * HALVES)
-            j1 = columns_of_out_ready((view + 1) * HALVES)
-            nc.vector.tensor_reduce(
-                out=out_sb[:, j0:j1],
-                in_=v[:, MERGE * j0 : MERGE * j1].rearrange("p (j t) -> p j t", t=MERGE),
-                axis=mybir.AxisListType.X, op=ADD,
-            )
-            nc.sync.dma_start(out=out[:, j0:j1], in_=out_sb[:, j0:j1])
+            for h in range(HALVES):
+                bank = view * HALVES + h
+                nc.scalar.activation(
+                    out=v[:, bank * BANK : (bank + 1) * BANK], in_=nm[h][:],
+                    func=mybir.ActivationFunctionType.Copy, scale=gate[:, 0:1],
+                )
+                j0 = columns_of_out_ready(bank)
+                j1 = columns_of_out_ready(bank + 1)
+                nc.vector.tensor_reduce(
+                    out=out_sb[:, j0:j1],
+                    in_=v[:, MERGE * j0 : MERGE * j1].rearrange("p (j t) -> p j t", t=MERGE),
+                    axis=mybir.AxisListType.X, op=ADD,
+                )
+                nc.sync.dma_start(out=out[:, j0:j1], in_=out_sb[:, j0:j1])

@@ -72,11 +72,12 @@ def tile_fusion_r3d_pa_kernel(
             nc.sync.dma_start(out=x_sb[view][:], in_=xs[view])
 
         def load_scales(w):
-            scale_rows = weights[w][1].bitcast(I32)
+            queue, view = (nc.gpsimd, F32) if w % 2 == 1 else (nc.sync, I32)
+            scale_rows = weights[w][1].bitcast(view)
             for quad in range(P // QUADRANT):
                 top = quad * QUADRANT
-                nc.sync.dma_start(
-                    out=w_scales[top : top + PASSES * SCALE_ROWS, w, :].bitcast(I32),
+                queue.dma_start(
+                    out=w_scales[top : top + PASSES * SCALE_ROWS, w, :].bitcast(view),
                     in_=scale_rows[:, quad * SCALE_ROWS : (quad + 1) * SCALE_ROWS, :],
                 )
 

@@ -27,6 +27,7 @@ WORDS_PASS = K_PASS // 2
 QUADRANT = 32
 SCALE_ROWS = 4
 STORE_STEP = 8
+SPACER_WIDTH = 16
 
 FLOPS = 2 * P * K * F * WEIGHTS
 
@@ -64,6 +65,7 @@ def tile_fusion_r3d_pa_kernel(
         w_scales = keep.tile([P, WEIGHTS, F], U8, align_bytes=64)
         v = keep.tile([P, VIEWS * F], F32)
         out_sb = keep.tile([P, F], F32)
+        spacer = keep.tile([P, VIEWS * (P // QUADRANT) * SPACER_WIDTH], BF16)
 
         make_identity(nc, ident[:])
         nc.vector.memset(w_scales[:].rearrange("p w n -> p (w n)").bitcast(I32), 0)
@@ -74,12 +76,21 @@ def tile_fusion_r3d_pa_kernel(
         def load_scales(w):
             queue, view = (nc.gpsimd, F32) if w % 2 == 1 else (nc.sync, I32)
             scale_rows = weights[w][1].bitcast(view)
-            for quad in range(P // QUADRANT):
+            spaced = w % 2 == 1
+            for place, quad in enumerate((0, 2, 1, 3) if spaced else (0, 1, 2, 3)):
                 top = quad * QUADRANT
                 queue.dma_start(
                     out=w_scales[top : top + PASSES * SCALE_ROWS, w, :].bitcast(view),
                     in_=scale_rows[:, quad * SCALE_ROWS : (quad + 1) * SCALE_ROWS, :],
                 )
+                if spaced:
+                    left = ((w // 2) * (P // QUADRANT) + place) * SPACER_WIDTH
+                    low = (place % 2) * 2 * QUADRANT + PASSES * SCALE_ROWS
+                    nc.gpsimd.dma_start(
+                        out=spacer[low : low + PASSES * SCALE_ROWS, left : left + SPACER_WIDTH],
+                        in_=xs[0][0 : PASSES * SCALE_ROWS, 0:SPACER_WIDTH]
+                        .rearrange("(i a) k -> a i k", a=PASSES),
+                    )
 
         def load_words(w):
             for g in range(PASSES):

@@ -93,6 +93,15 @@ def tile_fusion_r3d_pa_kernel(
                     )
 
         def load_words(w):
+            together = PASSES if w < WEIGHTS - 2 else 2 if w == WEIGHTS - 2 else 1
+            if together > 1:
+                for g in range(0, PASSES, together):
+                    nc.sync.dma_start(
+                        out=w_words[w][:, g : g + together, :].bitcast(I32),
+                        in_=weights[w][0][g : g + together]
+                        .rearrange("g p n t -> p g (n t)").bitcast(I32),
+                    )
+                return
             for g in range(PASSES):
                 is_last_load = w == WEIGHTS - 1 and g == PASSES - 1
                 width = BANK if is_last_load else F

from contextlib import ExitStack

import concourse.mybir as mybir
from concourse.masks import make_identity

F32 = mybir.dt.float32
BF16 = mybir.dt.bfloat16
I32 = mybir.dt.int32
U32 = mybir.dt.uint32
U8 = mybir.dt.uint8
FP8X4 = mybir.dt.float8_e4m3fn_x4
ADD = mybir.AluOpType.add
MULT = mybir.AluOpType.mult

P = 128
PACK = 4
K = 2048
K_PASS = P * PACK
PASSES = K // K_PASS
F = 1024
BANK = 512
HALVES = F // BANK
VIEWS = 3
WEIGHTS = 2 * VIEWS
MERGE = 3
WORDS_PASS = K_PASS // 2
QUADRANT = 32
SCALE_ROWS = 4
STORE_STEP = 8
SPACER_WIDTH = 16

FLOPS = 2 * P * K * F * WEIGHTS


def columns_of_out_ready(banks_done):
    return (banks_done * BANK // MERGE) // STORE_STEP * STORE_STEP


def tile_fusion_r3d_pa_kernel(
    tc,
    x_dash, x_rear, x_right,
    Wd_nm_words, Wd_nm_scales, Wd_an_words, Wd_an_scales,
    Wr_nm_words, Wr_nm_scales, Wr_an_words, Wr_an_scales,
    Wt_nm_words, Wt_nm_scales, Wt_an_words, Wt_an_scales,
    out,
):
    nc = tc.nc
    xs = [x_dash, x_rear, x_right]
    weights = [
        (Wd_an_words, Wd_an_scales), (Wd_nm_words, Wd_nm_scales),
        (Wr_an_words, Wr_an_scales), (Wr_nm_words, Wr_nm_scales),
        (Wt_an_words, Wt_an_scales), (Wt_nm_words, Wt_nm_scales),
    ]

    with ExitStack() as ctx:
        keep = ctx.enter_context(tc.tile_pool(name="keep", bufs=1))
        xt_pool = ctx.enter_context(tc.psum_pool(name="xt_pool", bufs=4))
        acc_pool = ctx.enter_context(tc.psum_pool(name="acc_pool", bufs=1))
        ctx.enter_context(tc.manual_schedule())

        ident = keep.tile([P, P], F32)
        x_sb = [keep.tile([P, K], BF16, name="x_sb%d" % view) for view in range(VIEWS)]
        w_words = [keep.tile([P, PASSES, F], U32, name="w_words%d" % w, align_bytes=64)
                   for w in range(WEIGHTS)]
        w_scales = keep.tile([P, WEIGHTS, F], U8, align_bytes=64)
        v = keep.tile([P, VIEWS * F], F32)
        out_sb = keep.tile([P, F], F32)
        spacer = keep.tile([P, VIEWS * (P // QUADRANT) * SPACER_WIDTH], BF16)

        make_identity(nc, ident[:])
        nc.vector.memset(w_scales[:].rearrange("p w n -> p (w n)").bitcast(I32), 0)

        def load_x(view):
            nc.sync.dma_start(out=x_sb[view][:], in_=xs[view])

        def load_scales(w):
            queue, view = (nc.gpsimd, F32) if w % 2 == 1 else (nc.sync, I32)
            scale_rows = weights[w][1].bitcast(view)
            spaced = w % 2 == 1
            for place, quad in enumerate((0, 2, 1, 3) if spaced else (0, 1, 2, 3)):
                top = quad * QUADRANT
                queue.dma_start(
                    out=w_scales[top : top + PASSES * SCALE_ROWS, w, :].bitcast(view),
                    in_=scale_rows[:, quad * SCALE_ROWS : (quad + 1) * SCALE_ROWS, :],
                )
                if spaced:
                    left = ((w // 2) * (P // QUADRANT) + place) * SPACER_WIDTH
                    low = (place % 2) * 2 * QUADRANT + PASSES * SCALE_ROWS
                    nc.gpsimd.dma_start(
                        out=spacer[low : low + PASSES * SCALE_ROWS, left : left + SPACER_WIDTH],
                        in_=xs[0][0 : PASSES * SCALE_ROWS, 0:SPACER_WIDTH]
                        .rearrange("(i a) k -> a i k", a=PASSES),
                    )

        def load_words(w):
            together = PASSES if w < WEIGHTS - 2 else 2 if w == WEIGHTS - 2 else 1
            if together > 1:
                for g in range(0, PASSES, together):
                    nc.sync.dma_start(
                        out=w_words[w][:, g : g + together, :].bitcast(I32),
                        in_=weights[w][0][g : g + together]
                        .rearrange("g p n t -> p g (n t)").bitcast(I32),
                    )
                return
            for g in range(PASSES):
                is_last_load = w == WEIGHTS - 1 and g == PASSES - 1
                width = BANK if is_last_load else F
                for left in range(0, F, width):
                    nc.sync.dma_start(
                        out=w_words[w][:, g, left : left + width].bitcast(I32),
                        in_=weights[w][0][g, :, left : left + width, :]
                        .rearrange("p n t -> p (n t)").bitcast(I32),
                    )

        load_x(0)
        load_scales(0)
        load_x(1)
        load_x(2)
        for w in range(WEIGHTS):
            if w + 1 < WEIGHTS:
                load_scales(w + 1)
            load_words(w)

        x_codes = []
        x_scales = []
        for view in range(VIEWS):
            x_words = x_sb[view][:].bitcast(F32)
            grouped = keep.tile([P, PASSES, P, PACK], BF16, name="grouped%d" % view, align_bytes=64)
            grouped_words = (
                grouped[:].rearrange("p g b t -> p (g b t)").bitcast(F32)
                .rearrange("p (g b u) -> p g b u", g=PASSES, u=2)
            )
            for pair in range(PASSES // 2):
                xt = xt_pool.tile([P, 2, 2, P], F32)
                for i in range(2):
                    g = 2 * pair + i
                    for u in range(2):
                        nc.tensor.transpose(
                            xt[:, i, u, :],
                            x_words[:, g * WORDS_PASS + u : (g + 1) * WORDS_PASS : 2],
                            ident[:],
                        )
                copy_out = nc.scalar.copy if pair == 0 else nc.vector.tensor_copy
                copy_out(
                    out=grouped_words[:, 2 * pair : 2 * pair + 2, :, :],
                    in_=xt[:].rearrange("p i u b -> p i b u"),
                )
            codes = keep.tile([P, PASSES * P], U32, name="x_codes%d" % view, align_bytes=64)
            scales = keep.tile([P, PASSES * P], U8, name="x_scales%d" % view, align_bytes=64)
            nc.vector.quantize_mx(
                out=codes[:].bitcast(FP8X4),
                scales=scales[:],
                in_=grouped[:].rearrange("p g b t -> p (g b t)"),
            )
            x_codes.append(codes)
            x_scales.append(scales)

        def multiply(view, w, tag):
            acc = [acc_pool.tile([P, BANK], F32, name="%s%d" % (tag, h)) for h in range(HALVES)]
            for g in range(PASSES):
                rows = slice(g * P, (g + 1) * P)
                for h in range(HALVES):
                    cols = slice(h * BANK, (h + 1) * BANK)
                    nc.tensor.matmul_mx(
                        out=acc[h][:],
                        lhsT=x_codes[view][:, rows].bitcast(FP8X4),
                        lhsT_scale=x_scales[view][:, rows],
                        rhs=w_words[w][:, g, cols].bitcast(FP8X4),
                        rhs_scale=w_scales[g * SCALE_ROWS : P, w, cols],
                        start=(g == 0),
                        stop=(g == PASSES - 1),
                    )
            return acc

        for view in range(VIEWS):
            an = multiply(view, 2 * view, "an")
            an_sum = keep.tile([P, HALVES], F32, name="an_sum%d" % view)
            for h in range(HALVES):
                nc.vector.tensor_reduce(
                    out=an_sum[:, h : h + 1], in_=an[h][:], axis=mybir.AxisListType.X, op=ADD
                )
            gate = keep.tile([P, 1], F32, name="gate%d" % view)
            nc.vector.tensor_scalar(
                out=gate[:], in0=an_sum[:, 0:1], scalar1=an_sum[:, 1:2],
                scalar2=1.0 / (F * MERGE), op0=ADD, op1=MULT,
            )

            nm = multiply(view, 2 * view + 1, "nm")
            for h in range(HALVES):
                bank = view * HALVES + h
                nc.scalar.activation(
                    out=v[:, bank * BANK : (bank + 1) * BANK], in_=nm[h][:],
                    func=mybir.ActivationFunctionType.Copy, scale=gate[:, 0:1],
                )
                j0 = columns_of_out_ready(bank)
                j1 = columns_of_out_ready(bank + 1)
                nc.vector.tensor_reduce(
                    out=out_sb[:, j0:j1],
                    in_=v[:, MERGE * j0 : MERGE * j1].rearrange("p (j t) -> p j t", t=MERGE),
                    axis=mybir.AxisListType.X, op=ADD,
                )
                nc.sync.dma_start(out=out[:, j0:j1], in_=out_sb[:, j0:j1])
